import numpy as np
import ml_dtypes


def mxq(x, axis, fmt="e4m3"):
    dtype, down = {"e4m3": (ml_dtypes.float8_e4m3fn, 7), "e5m2": (ml_dtypes.float8_e5m2, 14)}[fmt]
    v = np.moveaxis(np.asarray(x, np.float32).astype(ml_dtypes.bfloat16).astype(np.float64), axis, -1)
    blocks = v.reshape(v.shape[:-1] + (-1, 32))
    amax = np.abs(blocks).max(-1, keepdims=True)
    byte = np.maximum(np.where(amax > 0, np.frexp(amax)[1] - 1 + 127, 0) - down, 1)
    scale = np.exp2(byte - 127.0)
    codes = (blocks / scale).astype(np.float32).astype(dtype).astype(np.float64)
    return np.moveaxis((codes * scale).reshape(v.shape), -1, axis)


WIDE = False


def mx_kscale(k):
    if not WIDE:
        return np.ones(k)
    levels = np.array([18, -18])
    if k % 512:
        return np.exp2(np.random.permutation(np.resize(levels, k // 32))).repeat(32)
    a = np.empty((k // 512, 16))
    for p in range(k // 512):
        a[p, :8] = np.random.permutation(np.resize(levels, 8))
        for g in range(8):
            far = levels[np.abs(levels - a[p, g]) >= 10]
            a[p, g + 8] = far[np.random.randint(len(far))]
    return np.exp2(a.ravel()).repeat(32)


BF16 = ml_dtypes.bfloat16


def bf(x):
    return np.asarray(x, np.float32).astype(BF16)


def f64(x):
    return np.asarray(x).astype(np.float64)


B, R, G = 1024, 1024, 1024


def sigmoid(v):
    return 1.0 / (1.0 + np.exp(-v))


def setup_inputs():
    s = mx_kscale(B)[:, None]
    u = mx_kscale(G)
    y0 = bf(np.random.standard_normal((B, R)))
    z0 = bf(np.random.standard_normal((B, R)))
    dt = bf(0.3 + 0.2 * np.random.random(1))
    w10 = bf(np.random.standard_normal((G, R)) * 1.5 / np.sqrt(R))
    w20 = bf(np.random.standard_normal((G, R)) / np.sqrt(R))
    b1 = bf(np.random.standard_normal(G) * 0.3)
    b2 = bf(np.random.standard_normal(G) * 0.3)
    g = bf(np.random.standard_normal((B, G)) * np.exp2(np.random.randint(-6, 1, (B, 1))) * 4.0 / s * u)
    y_next = f64(y0) + f64(dt) * f64(z0)
    gate_pre = y_next @ f64(w10).T + f64(b1)
    value = y_next @ f64(w20).T + f64(b2)
    return {"y_tilde": bf(f64(y0) * s),
            "z_next": bf(f64(z0) * s),
            "dt": dt,
            "glu_w1": bf(f64(w10) / u[:, None]),
            "glu_w2": bf(f64(w20) / u[:, None]),
            "glu_b1": b1,
            "glu_b2": b2,
            "gate_pre": np.asarray(gate_pre, np.float32),
            "value": np.asarray(value, np.float32),
            "grad_out": g}


def reference(y_tilde, z_next, dt, glu_w1, glu_w2, glu_b1, glu_b2, gate_pre, value, grad_out):
    go = f64(grad_out)
    gate = sigmoid(f64(gate_pre))
    d1 = go * (f64(value) * gate * (1.0 - gate))
    d2 = go * gate
    y_next = f64(y_tilde) + f64(dt) * f64(z_next)
    dy = ((mxq(d1, 1, "e5m2") @ mxq(f64(glu_w1), 0, "e4m3"))
          + (mxq(d2, 1, "e5m2") @ mxq(f64(glu_w2), 0, "e4m3")))
    dw1 = mxq(d1, 0, "e5m2").T @ mxq(y_next, 0, "e4m3")
    return dy, dw1

@@ -1,0 +1,342 @@
+from contextlib import ExitStack
+
+import concourse.mybir as mybir
+from concourse.masks import make_identity
+
+B, R, G = 1024, 1024, 1024
+FLOPS = 3 * 2 * B * R * G
+BYTES = 5 * B * G * 2 + 2 * B * G * 4 + 2 * B * R * 4 + 2
+
+F32 = mybir.dt.float32
+BF16 = mybir.dt.bfloat16
+U32 = mybir.dt.uint32
+U8 = mybir.dt.uint8
+E4X4 = mybir.dt.float8_e4m3fn_x4
+E5X4 = mybir.dt.float8_e5m2_x4
+ALU = mybir.AluOpType
+ACT = mybir.ActivationFunctionType
+
+P = 128
+PACK = 4
+HALF = 512
+CHUNKS = 8
+
+
+def tile_instrumentedlocmblock_pb_v_kernel(
+    tc, y_tilde, z_next, dt, glu_w1, glu_w2, glu_b1, glu_b2, gate_pre, value, grad_out, out_0, out_1
+):
+    nc = tc.nc
+    with ExitStack() as ctx:
+        keep = ctx.enter_context(tc.tile_pool(name="keep", bufs=1))
+        load = ctx.enter_context(tc.tile_pool(name="load", bufs=3))
+        work = ctx.enter_context(tc.tile_pool(name="work", bufs=2))
+        psum = ctx.enter_context(tc.psum_pool(name="psum", bufs=4))
+        ctx.enter_context(tc.manual_schedule())
+
+        ident = keep.tile([P, P], F32, name="ident")
+        make_identity(nc, ident[:])
+        dt_col = keep.tile([P, 1], BF16, name="dt_col")
+        warm = keep.tile([P, 1], F32, name="warm")
+
+        copiers = {"V": nc.vector.tensor_copy, "S": nc.scalar.copy}
+        tiles = {}
+
+        def token_rows(tensor, half):
+            return tensor[half * HALF:(half + 1) * HALF, :].rearrange("(p j) w -> p (j w)", j=PACK)
+
+        def load_rows(name, tensor, dtype, c, count):
+            pair = c // 2
+            if (name, pair) not in tiles:
+                tiles[name, pair] = load.tile([P, 2 * G], dtype, name=name)
+            j = c % PACK
+            nc.sync.dma_start(
+                out=tiles[name, pair][:, (c % 2) * G:(c % 2 + count) * G],
+                in_=token_rows(tensor, c // PACK)[:, j * G:(j + count) * G],
+            )
+
+        def rows(name, c):
+            return tiles[name, c // 2][:, (c % 2) * G:(c % 2 + 1) * G]
+
+        def load_raw(name, tensor, half):
+            tiles[name, half] = load.tile([P, PACK * R], BF16, name="raw", bufs=5)
+            nc.sync.dma_start(out=tiles[name, half][:], in_=token_rows(tensor, half))
+
+        def raw_cols(name, half, r):
+            return tiles[name, half][:].rearrange("p (j w) -> p j w", j=PACK)[:, :, r * HALF:(r + 1) * HALF]
+
+        def new_mx(key, width, pool, tag, bufs):
+            codes = pool.tile([P, width], U32, name=tag + "_codes", bufs=bufs, align_bytes=64)
+            scales = pool.tile([P, width], U8, name=tag + "_scales", bufs=bufs, align_bytes=64)
+            tiles[key] = (codes, scales)
+
+        def sigmoid(c):
+            tiles["gate", c] = work.tile([P, G], F32, name="gate")
+            nc.scalar.activation(out=tiles["gate", c][:], in_=rows("x", c), func=ACT.Sigmoid)
+
+        def paired(ap):
+            return ap.rearrange("p (w u i) -> p u w i", u=2, i=2)
+
+        def make_d2(c):
+            tiles["d2", c] = work.tile([P, G], F32, name="d2")
+            nc.vector.tensor_tensor(
+                out=tiles["d2", c][:].rearrange("p (u w i) -> p u w i", u=2, i=2),
+                in0=paired(tiles["gate", c][:]), in1=paired(rows("go", c)), op=ALU.mult)
+
+        def make_slope(c):
+            tiles["slope", c] = work.tile([P, G], F32, name="slope", bufs=1)
+            nc.vector.scalar_tensor_tensor(
+                out=tiles["slope", c][:], in0=tiles["gate", c][:], scalar=1.0, in1=rows("v", c),
+                op0=ALU.subtract, op1=ALU.mult)
+
+        def make_d1(c):
+            half, j = divmod(c, PACK)
+            if j == 0:
+                tiles["d1", half] = work.tile([P, PACK * G], BF16, name="d1")
+            for u in range(2):
+                nc.vector.scalar_tensor_tensor(
+                    out=tiles["d1", half][:, j * G + u * HALF:j * G + (u + 1) * HALF].rearrange("p (w i) -> p w i", i=2),
+                    in0=paired(tiles["slope", c][:])[:, u], scalar=-1.0,
+                    in1=tiles["d2", c][:, u * HALF:(u + 1) * HALF].rearrange("p (w i) -> p w i", i=2),
+                    op0=ALU.mult, op1=ALU.mult)
+
+        def turn_d2(c, g):
+            bank = psum.tile([P, HALF], F32, name="turn")
+            tiles["turn2", c, g] = bank
+            for t in range(PACK):
+                u, i = divmod(t, 2)
+                first = u * HALF + g * 2 * P + i
+                nc.tensor.transpose(bank[:, t * P:(t + 1) * P], tiles["d2", c][:, first:first + 2 * P - i:2], ident[:])
+
+        def turn_d1(c):
+            half, j = divmod(c, PACK)
+            bank = psum.tile([P, HALF], F32, name="turn")
+            tiles["turn1", c] = bank
+            words = tiles["d1", half][:, j * G:(j + 1) * G].bitcast(F32)
+            for g in range(2):
+                for u in range(2):
+                    nc.tensor.transpose(bank[:, (2 * g + u) * P:(2 * g + u + 1) * P],
+                                        words[:, (2 * u + g) * P:(2 * u + g + 1) * P], ident[:])
+
+        def turned(c):
+            if ("turned", c) not in tiles:
+                tiles["turned", c] = work.tile([P, 2 * G], BF16, name="turned", align_bytes=64)
+            return tiles["turned", c]
+
+        def empty_d2(c, g, eng="S"):
+            copiers[eng](
+                out=turned(c)[:, G + g * HALF:G + (g + 1) * HALF].rearrange("p (n t) -> p n t", t=PACK),
+                in_=tiles["turn2", c, g][:].rearrange("p (t n) -> p n t", t=PACK))
+
+        def empty_d1(c, eng="S"):
+            copiers[eng](
+                out=turned(c)[:, 0:G].bitcast(F32).rearrange("p (g n u) -> p g n u", g=2, u=2),
+                in_=tiles["turn1", c][:].rearrange("p (g u n) -> p g n u", g=2, u=2))
+
+        def quantise(key, cols, fmt, source):
+            codes, scales = tiles[key]
+            nc.vector.quantize_mx(out=codes[:, cols].bitcast(fmt), scales=scales[:, cols], in_=source)
+
+        def quant_feature(c):
+            new_mx(("dT", c), HALF, work, "dT", 4)
+            quantise(("dT", c), slice(0, HALF), E5X4, turned(c)[:])
+
+        def weave(name, half, r, eng):
+            woven = work.tile([P, PACK * HALF], BF16, name="woven", bufs=4, align_bytes=64)
+            tiles["woven", name, half, r] = woven
+            copiers[eng](
+                out=woven[:].rearrange("p (c i j) -> p c j i", i=4, j=PACK),
+                in_=raw_cols(name, half, r).rearrange("p j (c i) -> p c j i", i=4))
+
+        def quant_e4(name, half, r):
+            new_mx((name, half, r), HALF, keep, "%s_%d_%d" % (name, half, r), 1)
+            quantise((name, half, r), slice(0, HALF), E4X4, tiles["woven", name, half, r][:])
+
+        def make_y(half, r):
+            nc.vector.scalar_tensor_tensor(
+                out=raw_cols("y", half, r), in0=raw_cols("z", half, r), scalar=dt_col[:],
+                in1=raw_cols("y", half, r), op0=ALU.mult, op1=ALU.add)
+
+        def weave_d1(half, g, eng="V"):
+            woven = work.tile([P, PACK * HALF], BF16, name="woven", bufs=4, align_bytes=64)
+            tiles["woven", "d1", half, g] = woven
+            copiers[eng](
+                out=woven[:].rearrange("p (w u i j) -> p u w j i", u=2, i=2, j=PACK),
+                in_=tiles["d1", half][:].rearrange("p (j u g w i) -> p g u w j i", j=PACK, u=2, g=2, i=2)[:, g])
+
+        def quant_d1(half, g):
+            if g == 0:
+                new_mx(("d1q", half), G, keep, "d1q_%d" % half, 1)
+            quantise(("d1q", half), slice(g * HALF, (g + 1) * HALF), E5X4, tiles["woven", "d1", half, g][:])
+
+        def product(key, passes, tag="acc", first=0, stop=None):
+            if first == 0:
+                tiles[key] = psum.tile([P, HALF], F32, name=tag)
+            acc = tiles[key]
+            for n, (left, block, right) in list(enumerate(passes))[first:stop]:
+                cols = slice(block * P, (block + 1) * P)
+                nc.tensor.matmul_mx(
+                    out=acc[:], lhsT=tiles[left][0][:, cols].bitcast(E5X4), lhsT_scale=tiles[left][1][:, cols],
+                    rhs=tiles[right][0][:].bitcast(E4X4), rhs_scale=tiles[right][1][:],
+                    start=(n == 0), stop=(n == len(passes) - 1))
+
+        def product_0(c, r):
+            product(("acc0", c, r), [(("dT", c), 2 * m + g, (name, g, r))
+                                     for m, name in enumerate(("w1", "w2")) for g in range(2)])
+
+        def product_1(m, r, tag="acc", first=0, stop=None):
+            product(("acc1", m, r), [(("d1q", half), m, ("y", half, r)) for half in range(2)], tag, first, stop)
+
+        def empty_0(c, r, eng="S"):
+            if r == 0:
+                tiles["res0", c] = work.tile([P, R], F32, name="result", bufs=4)
+            copiers[eng](out=tiles["res0", c][:, r * HALF:(r + 1) * HALF], in_=tiles["acc0", c, r][:])
+            if r == 1:
+                half, j = divmod(c, PACK)
+                nc.sync.dma_start(out=token_rows(out_0, half)[:, j * R:(j + 1) * R], in_=tiles["res0", c][:])
+
+        def empty_1(m, r, eng):
+            if m % 2 == 0:
+                tiles["res1", m // 2, r] = work.tile([P, R], F32, name="result", bufs=4)
+            res = tiles["res1", m // 2, r]
+            copiers[eng](out=res[:, (m % 2) * HALF:(m % 2 + 1) * HALF], in_=tiles["acc1", m, r][:])
+            if m % 2 == 1:
+                nc.sync.dma_start(
+                    out=out_1.rearrange("(m p) w -> p m w", p=P)[:, m - 1:m + 1, r * HALF:(r + 1) * HALF],
+                    in_=res[:].rearrange("p (m w) -> p m w", m=2))
+
+        def out_0_tile(c):
+            for r in range(2):
+                product_0(c, r)
+
+        def out_0_empty(c):
+            for r in range(2):
+                empty_0(c, r)
+
+
+        def load_chunks(c, count):
+            load_rows("x", gate_pre, F32, c, count)
+            if c % 2 == 0:
+                load_rows("go", grad_out, BF16, c, 2)
+            load_rows("v", value, F32, c, count)
+        W = lambda name, g, r, eng: (lambda: weave(name, g, r, eng))
+        Q = lambda name, g, r: (lambda: quant_e4(name, g, r))
+        L = lambda name, t, h: (lambda: load_raw(name, t, h))
+        LC = lambda c, n: (lambda: load_chunks(c, n))
+        Y = lambda h, r: (lambda: make_y(h, r))
+        WD = lambda h, g, eng="V": (lambda: weave_d1(h, g, eng))
+        QD = lambda h, g: (lambda: quant_d1(h, g))
+        M0 = lambda c: (lambda: out_0_tile(c))
+        E0 = lambda c: (lambda: out_0_empty(c))
+        def run(steps):
+            for step in steps:
+                step()
+
+        H = lambda c, r, eng="S": (lambda: (product_0(c, r), empty_0(c, r, eng)))
+        nc.scalar.activation(out=warm[:], in_=ident[:, 0:1], func=ACT.Sigmoid)
+        load_chunks(0, 1)
+        load_rows("x", gate_pre, F32, 1, 1)
+        load_raw("w1", glu_w1, 0)
+        load_rows("v", value, F32, 1, 1)
+        load_rows("x", gate_pre, F32, 2, 1)
+        load_raw("w2", glu_w2, 0)
+        load_rows("go", grad_out, BF16, 2, 2)
+        load_rows("v", value, F32, 2, 1)
+        load_rows("x", gate_pre, F32, 3, 1)
+        load_raw("w1", glu_w1, 1)
+        load_rows("v", value, F32, 3, 1)
+        load_rows("x", gate_pre, F32, 4, 2)
+        load_raw("w2", glu_w2, 1)
+        load_rows("go", grad_out, BF16, 4, 2)
+        load_rows("v", value, F32, 4, 2)
+        nc.sync.dma_start(out=dt_col[:], in_=dt.partition_broadcast(P))
+        load_raw("y", y_tilde, 0)
+
+        pre = {
+            1: [W("w1", 0, 0, "S")],
+            3: [W("w1", 1, 0, "S")],
+        }
+        post = {
+            1: [W("w2", 0, 0, "S")],
+            2: [W("w2", 0, 1, "S")],
+            3: [W("w2", 1, 1, "S")],
+            4: [H(0, 0), H(0, 1), H(1, 0), H(1, 1)],
+            5: [H(2, 0), H(2, 1), H(3, 0), H(3, 1)],
+            6: [W("y", 0, 0, "S"), H(4, 0), H(4, 1)],
+            7: [H(5, 0), H(5, 1), W("y", 1, 0, "S")],
+        }
+        between = {
+            1: [W("w1", 0, 1, "V")],
+            7: [lambda: quant_feature(6)],
+        }
+        spacer = {
+            1: [Q("w1", 0, 1)],
+            2: [Q("w2", 0, 0)],
+            3: [W("w1", 1, 1, "V"), Q("w2", 0, 1), L("y", y_tilde, 1)],
+            4: [WD(0, 0)],
+            5: [QD(0, 0)],
+            6: [WD(0, 1)],
+            7: [Q("y", 0, 0)],
+        }
+        end = {
+            1: [Q("w1", 0, 0), L("z", z_next, 0), LC(6, 2)],
+            3: [W("w2", 1, 0, "V"), Q("w1", 1, 0), Q("w1", 1, 1), L("z", z_next, 1), Q("w2", 1, 0), Q("w2", 1, 1)],
+            5: [Y(0, 0)],
+            6: [QD(0, 1), Y(1, 0)],
+        }
+        sigmoid(0)
+        for c in range(CHUNKS):
+            if c > 0:
+                turn_d1(c - 1)
+                empty_d2(c - 1, 0)
+                empty_d2(c - 1, 1)
+                empty_d1(c - 1)
+            run(pre.get(c, []))
+            if c + 1 < CHUNKS:
+                sigmoid(c + 1)
+            make_d2(c)
+            run(between.get(c, []))
+            make_slope(c)
+            run(spacer.get(c, []))
+            run(post.get(c, []))
+            turn_d2(c, 0)
+            turn_d2(c, 1)
+            make_d1(c)
+            if 0 < c < 7:
+                quant_feature(c - 1)
+            run(end.get(c, []))
+        last = CHUNKS - 1
+        out_0_tile(last - 1)
+        empty_d2(last, 0)
+        empty_d2(last, 1)
+        turn_d1(last)
+        empty_d1(last)
+        weave_d1(1, 0)
+        quant_e4("y", 1, 0)
+        quant_d1(1, 0)
+        quant_feature(last)
+        out_0_empty(last - 1)
+        for m in range(4):
+            product_1(m, 0, "turn")
+        make_y(0, 1)
+        weave_d1(1, 1)
+        for m in range(4):
+            empty_1(m, 0, "S")
+        out_0_tile(last)
+        make_y(1, 1)
+        quant_d1(1, 1)
+        weave("y", 0, 1, "S")
+        out_0_empty(last)
+        weave("y", 1, 1, "V")
+        quant_e4("y", 0, 1)
+        for m in range(4, 8):
+            product_1(m, 0, "turn")
+            empty_1(m, 0, "S")
+        for m in range(4):
+            product_1(m, 1, "acc", 0, 1)
+        quant_e4("y", 1, 1)
+        for m in range(4):
+            product_1(m, 1, "acc", 1)
+            empty_1(m, 1, "VS"[m % 2])
+        for m in range(4, 8):
+            product_1(m, 1, "turn")
+            empty_1(m, 1, "VS"[m % 2])

@@ -20,6 +20,8 @@ P = 128
 PACK = 4
 HALF = 512
 CHUNKS = 8
+PARTS = [(0, 1), (1, 1), (2, 2), (4, 2), (6, 2)]
+PART_OF = [0, 1, 2, 2, 3, 3, 4, 4]
 
 
 def tile_instrumentedlocmblock_pb_v_kernel(
@@ -35,7 +37,9 @@ def tile_instrumentedlocmblock_pb_v_kernel(
 
         ident = keep.tile([P, P], F32, name="ident")
         make_identity(nc, ident[:])
-        dt_col = keep.tile([P, 1], BF16, name="dt_col")
+        dt_raw = keep.tile([P, 1], BF16, name="dt_raw")
+        dt_first = keep.tile([P, 1], F32, name="dt_first")
+        dt_col = keep.tile([P, 1], F32, name="dt_col")
         warm = keep.tile([P, 1], F32, name="warm")
 
         copiers = {"V": nc.vector.tensor_copy, "S": nc.scalar.copy}
@@ -69,6 +73,15 @@ def tile_instrumentedlocmblock_pb_v_kernel(
             scales = pool.tile([P, width], U8, name=tag + "_scales", bufs=bufs, align_bytes=64)
             tiles[key] = (codes, scales)
 
+        def spread_dt():
+            nc.scalar.copy(out=dt_first[:], in_=dt_raw[:])
+            bank = psum.tile([P, HALF], F32, name="acc")
+            nc.tensor.transpose(bank[:, 0:P], dt_first[:].to_broadcast([P, P]), ident[:])
+            tiles["dt_bank"] = bank
+
+        def take_dt():
+            nc.scalar.copy(out=dt_col[:], in_=tiles["dt_bank"][:, 0:1])
+
         def sigmoid(c):
             tiles["gate", c] = work.tile([P, G], F32, name="gate")
             nc.scalar.activation(out=tiles["gate", c][:], in_=rows("x", c), func=ACT.Sigmoid)
@@ -79,7 +92,7 @@ def tile_instrumentedlocmblock_pb_v_kernel(
         def make_d2(c):
             tiles["d2", c] = work.tile([P, G], F32, name="d2")
             nc.vector.tensor_tensor(
-                out=tiles["d2", c][:].rearrange("p (u w i) -> p u w i", u=2, i=2),
+                out=tiles["d2", c][:].rearrange("p (u i w) -> p u w i", u=2, i=2),
                 in0=paired(tiles["gate", c][:]), in1=paired(rows("go", c)), op=ALU.mult)
 
         def make_slope(c):
@@ -96,16 +109,15 @@ def tile_instrumentedlocmblock_pb_v_kernel(
                 nc.vector.scalar_tensor_tensor(
                     out=tiles["d1", half][:, j * G + u * HALF:j * G + (u + 1) * HALF].rearrange("p (w i) -> p w i", i=2),
                     in0=paired(tiles["slope", c][:])[:, u], scalar=-1.0,
-                    in1=tiles["d2", c][:, u * HALF:(u + 1) * HALF].rearrange("p (w i) -> p w i", i=2),
+                    in1=tiles["d2", c][:, u * HALF:(u + 1) * HALF].rearrange("p (i w) -> p w i", i=2),
                     op0=ALU.mult, op1=ALU.mult)
 
         def turn_d2(c, g):
             bank = psum.tile([P, HALF], F32, name="turn")
             tiles["turn2", c, g] = bank
             for t in range(PACK):
-                u, i = divmod(t, 2)
-                first = u * HALF + g * 2 * P + i
-                nc.tensor.transpose(bank[:, t * P:(t + 1) * P], tiles["d2", c][:, first:first + 2 * P - i:2], ident[:])
+                first = (2 * t + g) * P
+                nc.tensor.transpose(bank[:, t * P:(t + 1) * P], tiles["d2", c][:, first:first + P], ident[:])
 
         def turn_d1(c):
             half, j = divmod(c, PACK)
@@ -136,9 +148,10 @@ def tile_instrumentedlocmblock_pb_v_kernel(
             codes, scales = tiles[key]
             nc.vector.quantize_mx(out=codes[:, cols].bitcast(fmt), scales=scales[:, cols], in_=source)
 
-        def quant_feature(c):
-            new_mx(("dT", c), HALF, work, "dT", 4)
-            quantise(("dT", c), slice(0, HALF), E5X4, turned(c)[:])
+        def quant_feature(c, first=0, count=2):
+            if ("dT", c) not in tiles:
+                new_mx(("dT", c), HALF, work, "dT", 4)
+            quantise(("dT", c), slice(first * 256, (first + count) * 256), E5X4, turned(c)[:, first * G:(first + count) * G])
 
         def weave(name, half, r, eng):
             woven = work.tile([P, PACK * HALF], BF16, name="woven", bufs=4, align_bytes=64)
@@ -151,22 +164,39 @@ def tile_instrumentedlocmblock_pb_v_kernel(
             new_mx((name, half, r), HALF, keep, "%s_%d_%d" % (name, half, r), 1)
             quantise((name, half, r), slice(0, HALF), E4X4, tiles["woven", name, half, r][:])
 
-        def make_y(half, r):
-            nc.vector.scalar_tensor_tensor(
-                out=raw_cols("y", half, r), in0=raw_cols("z", half, r), scalar=dt_col[:],
-                in1=raw_cols("y", half, r), op0=ALU.mult, op1=ALU.add)
+        def make_y(half, r, h):
+            if h == 0:
+                tiles["y_pairs", half, r] = work.tile([P, PACK * HALF], BF16, name="y_pairs", bufs=2)
+            pairs = tiles["y_pairs", half, r]
+            if True:
+                nc.vector.scalar_tensor_tensor(
+                    out=pairs[:, h * G:(h + 1) * G].rearrange("p (c e) -> p c e", e=2),
+                    in0=raw_cols("z", half, r)[:, 2 * h:2 * h + 2, :].rearrange("p e c -> p c e"), scalar=dt_col[:],
+                    in1=raw_cols("y", half, r)[:, 2 * h:2 * h + 2, :].rearrange("p e c -> p c e"),
+                    op0=ALU.mult, op1=ALU.add)
 
-        def weave_d1(half, g, eng="V"):
+        def weave_y(half, r, eng):
             woven = work.tile([P, PACK * HALF], BF16, name="woven", bufs=4, align_bytes=64)
-            tiles["woven", "d1", half, g] = woven
+            tiles["woven", "y", half, r] = woven
             copiers[eng](
-                out=woven[:].rearrange("p (w u i j) -> p u w j i", u=2, i=2, j=PACK),
-                in_=tiles["d1", half][:].rearrange("p (j u g w i) -> p g u w j i", j=PACK, u=2, g=2, i=2)[:, g])
+                out=woven[:].bitcast(F32).rearrange("p (c h) -> p c h", h=2),
+                in_=tiles["y_pairs", half, r][:].bitcast(F32).rearrange("p (h c) -> p c h", h=2))
 
-        def quant_d1(half, g):
-            if g == 0:
-                new_mx(("d1q", half), G, keep, "d1q_%d" % half, 1)
-            quantise(("d1q", half), slice(g * HALF, (g + 1) * HALF), E5X4, tiles["woven", "d1", half, g][:])
+        def weave_d1(half, part, eng="V"):
+            first, count = PARTS[part]
+            if ("woven", "d1", part) not in tiles:
+                tiles["woven", "d1", part] = work.tile([P, PACK * HALF], BF16, name="woven", bufs=4, align_bytes=64)
+            width = count * HALF
+            copiers[eng](
+                out=tiles["woven", "d1", part][:, half * width:(half + 1) * width].rearrange("p (w u i j) -> p u w j i", u=2, i=2, j=PACK),
+                in_=tiles["d1", half][:].rearrange("p (j u w i) -> p u w j i", j=PACK, u=2, i=2)[:, :, first * 32:(first + count) * 32])
+
+        def quant_d1(part, half=0, halves=2):
+            if ("d1q", part) not in tiles:
+                new_mx(("d1q", part), HALF, work, "d1q", 3)
+            count = PARTS[part][1]
+            quantise(("d1q", part), slice(half * count * P, (half + halves) * count * P), E5X4,
+                     tiles["woven", "d1", part][:, half * count * HALF:(half + halves) * count * HALF])
 
         def product(key, passes, tag="acc", first=0, stop=None):
             if first == 0:
@@ -179,12 +209,12 @@ def tile_instrumentedlocmblock_pb_v_kernel(
                     rhs=tiles[right][0][:].bitcast(E4X4), rhs_scale=tiles[right][1][:],
                     start=(n == 0), stop=(n == len(passes) - 1))
 
-        def product_0(c, r):
+        def product_0(c, r, first=0, stop=None):
             product(("acc0", c, r), [(("dT", c), 2 * m + g, (name, g, r))
-                                     for m, name in enumerate(("w1", "w2")) for g in range(2)])
+                                     for m, name in ((1, "w2"), (0, "w1")) for g in range(2)], "acc", first, stop)
 
         def product_1(m, r, tag="acc", first=0, stop=None):
-            product(("acc1", m, r), [(("d1q", half), m, ("y", half, r)) for half in range(2)], tag, first, stop)
+            product(("acc1", m, r), [(("d1q", PART_OF[m]), PARTS[PART_OF[m]][1] * half + m - PARTS[PART_OF[m]][0], ("y", half, r)) for half in range(2)], tag, first, stop)
 
         def empty_0(c, r, eng="S"):
             if r == 0:
@@ -195,14 +225,12 @@ def tile_instrumentedlocmblock_pb_v_kernel(
                 nc.sync.dma_start(out=token_rows(out_0, half)[:, j * R:(j + 1) * R], in_=tiles["res0", c][:])
 
         def empty_1(m, r, eng):
-            if m % 2 == 0:
-                tiles["res1", m // 2, r] = work.tile([P, R], F32, name="result", bufs=4)
-            res = tiles["res1", m // 2, r]
-            copiers[eng](out=res[:, (m % 2) * HALF:(m % 2 + 1) * HALF], in_=tiles["acc1", m, r][:])
-            if m % 2 == 1:
-                nc.sync.dma_start(
-                    out=out_1.rearrange("(m p) w -> p m w", p=P)[:, m - 1:m + 1, r * HALF:(r + 1) * HALF],
-                    in_=res[:].rearrange("p (m w) -> p m w", m=2))
+            if r == 0:
+                tiles["res1", m] = work.tile([P, R], F32, name="result", bufs=4)
+            res = tiles["res1", m]
+            copiers[eng](out=res[:, r * HALF:(r + 1) * HALF], in_=tiles["acc1", m, r][:])
+            if r == 1:
+                nc.sync.dma_start(out=out_1[m * P:(m + 1) * P, :], in_=res[:])
 
         def out_0_tile(c):
             for r in range(2):
@@ -222,9 +250,9 @@ def tile_instrumentedlocmblock_pb_v_kernel(
         Q = lambda name, g, r: (lambda: quant_e4(name, g, r))
         L = lambda name, t, h: (lambda: load_raw(name, t, h))
         LC = lambda c, n: (lambda: load_chunks(c, n))
-        Y = lambda h, r: (lambda: make_y(h, r))
+        Y = lambda t, r, h: (lambda: make_y(t, r, h))
         WD = lambda h, g, eng="V": (lambda: weave_d1(h, g, eng))
-        QD = lambda h, g: (lambda: quant_d1(h, g))
+        QD = lambda g: (lambda: quant_d1(g))
         M0 = lambda c: (lambda: out_0_tile(c))
         E0 = lambda c: (lambda: out_0_empty(c))
         def run(steps):
@@ -232,10 +260,18 @@ def tile_instrumentedlocmblock_pb_v_kernel(
                 step()
 
         H = lambda c, r, eng="S": (lambda: (product_0(c, r), empty_0(c, r, eng)))
-        nc.scalar.activation(out=warm[:], in_=ident[:, 0:1], func=ACT.Sigmoid)
-        load_chunks(0, 1)
-        load_rows("x", gate_pre, F32, 1, 1)
+        WY = lambda h, r: (lambda: weave_y(h, r, "S"))
+        LR = lambda name, t, d, c, n: (lambda: load_rows(name, t, d, c, n))
+
+        load_rows("x", gate_pre, F32, 0, 1)
+        load_rows("go", grad_out, BF16, 0, 1)
         load_raw("w1", glu_w1, 0)
+        load_rows("v", value, F32, 0, 1)
+        nc.gpsimd.memset(dt_raw[:], 0.0)
+        nc.scalar.dma_start(out=dt_raw[0:1, :], in_=dt.unsqueeze(0))
+        nc.scalar.activation(out=warm[:], in_=ident[:, 0:1], func=ACT.Sigmoid)
+        load_rows("x", gate_pre, F32, 1, 1)
+        load_rows("go", grad_out, BF16, 1, 1)
         load_rows("v", value, F32, 1, 1)
         load_rows("x", gate_pre, F32, 2, 1)
         load_raw("w2", glu_w2, 0)
@@ -247,48 +283,52 @@ def tile_instrumentedlocmblock_pb_v_kernel(
         load_rows("x", gate_pre, F32, 4, 2)
         load_raw("w2", glu_w2, 1)
         load_rows("go", grad_out, BF16, 4, 2)
-        load_rows("v", value, F32, 4, 2)
-        nc.sync.dma_start(out=dt_col[:], in_=dt.partition_broadcast(P))
+        load_rows("v", value, F32, 4, 1)
         load_raw("y", y_tilde, 0)
-
         pre = {
-            1: [W("w1", 0, 0, "S")],
-            3: [W("w1", 1, 0, "S")],
+            0: [W("w1", 0, 1, "S")],
+            1: [take_dt],
+            3: [W("w1", 1, 1, "S")],
+            5: [WY(0, 0)],
+            7: [WY(1, 1)],
         }
         post = {
             1: [W("w2", 0, 0, "S")],
-            2: [W("w2", 0, 1, "S")],
+            2: [W("w2", 0, 1, "S"), L("y", y_tilde, 1), W("w1", 1, 0, "S")],
             3: [W("w2", 1, 1, "S")],
-            4: [H(0, 0), H(0, 1), H(1, 0), H(1, 1)],
-            5: [H(2, 0), H(2, 1), H(3, 0), H(3, 1)],
-            6: [W("y", 0, 0, "S"), H(4, 0), H(4, 1)],
-            7: [H(5, 0), H(5, 1), W("y", 1, 0, "S")],
+            4: [H(0, 0), H(1, 0), H(0, 1), H(1, 1)],
+            5: [H(2, 0), H(2, 1), WY(0, 1), H(3, 0), H(3, 1)],
+            6: [WY(1, 0), H(4, 0), H(4, 1), WD(0, 0, "S"), WD(0, 1, "S")],
+            7: [H(5, 0), H(5, 1)],
         }
         between = {
-            1: [W("w1", 0, 1, "V")],
+            0: [W("w1", 0, 0, "V")],
             7: [lambda: quant_feature(6)],
         }
         spacer = {
-            1: [Q("w1", 0, 1)],
+            0: [Q("w1", 0, 0)],
             2: [Q("w2", 0, 0)],
-            3: [W("w1", 1, 1, "V"), Q("w2", 0, 1), L("y", y_tilde, 1)],
-            4: [WD(0, 0)],
-            5: [QD(0, 0)],
-            6: [WD(0, 1)],
-            7: [Q("y", 0, 0)],
+            3: [Q("w2", 0, 1)],
+            4: [Q("w2", 1, 1), Y(0, 0, 0)],
+            5: [Y(0, 1, 1)],
+            6: [Q("y", 0, 1)],
+            7: [Q("y", 1, 1)],
         }
         end = {
-            1: [Q("w1", 0, 0), L("z", z_next, 0), LC(6, 2)],
-            3: [W("w2", 1, 0, "V"), Q("w1", 1, 0), Q("w1", 1, 1), L("z", z_next, 1), Q("w2", 1, 0), Q("w2", 1, 1)],
-            5: [Y(0, 0)],
-            6: [QD(0, 1), Y(1, 0)],
+            0: [Q("w1", 0, 1), spread_dt, L("z", z_next, 0), LR("v", value, F32, 5, 1)],
+            1: [LR("x", gate_pre, F32, 6, 2)],
+            3: [Q("w1", 1, 0), W("w2", 1, 0, "V"), Q("w1", 1, 1), L("z", z_next, 1), LR("go", grad_out, BF16, 6, 2), LR("v", value, F32, 6, 2), Q("w2", 1, 0)],
+            4: [Y(0, 0, 1), Y(0, 1, 0)],
+            5: [Q("y", 0, 0), Y(1, 0, 0), Y(1, 0, 1)],
+            6: [Y(1, 1, 0), Y(1, 1, 1), Q("y", 1, 0)],
         }
         sigmoid(0)
         for c in range(CHUNKS):
             if c > 0:
                 turn_d1(c - 1)
-                empty_d2(c - 1, 0)
-                empty_d2(c - 1, 1)
+                if c < 7:
+                    empty_d2(c - 1, 0)
+                    empty_d2(c - 1, 1)
                 empty_d1(c - 1)
             run(pre.get(c, []))
             if c + 1 < CHUNKS:
@@ -300,43 +340,53 @@ def tile_instrumentedlocmblock_pb_v_kernel(
             run(post.get(c, []))
             turn_d2(c, 0)
             turn_d2(c, 1)
+            if c >= 6:
+                empty_d2(c, 0)
+                empty_d2(c, 1)
+            if c == 7:
+                out_0_tile(6)
             make_d1(c)
             if 0 < c < 7:
                 quant_feature(c - 1)
             run(end.get(c, []))
         last = CHUNKS - 1
-        out_0_tile(last - 1)
-        empty_d2(last, 0)
-        empty_d2(last, 1)
         turn_d1(last)
+        out_0_empty(last - 1)
+        quant_feature(last, 1, 1)
         empty_d1(last)
         weave_d1(1, 0)
-        quant_e4("y", 1, 0)
-        quant_d1(1, 0)
-        quant_feature(last)
-        out_0_empty(last - 1)
-        for m in range(4):
-            product_1(m, 0, "turn")
-        make_y(0, 1)
         weave_d1(1, 1)
-        for m in range(4):
-            empty_1(m, 0, "S")
-        out_0_tile(last)
-        make_y(1, 1)
-        quant_d1(1, 1)
-        weave("y", 0, 1, "S")
+        for r in range(2):
+            product_0(last, r, 0, 2)
+        quant_d1(0)
+        quant_d1(1)
+        for m in range(2):
+            for r in range(2):
+                product_1(m, r, "turn")
+        quant_feature(last, 0, 1)
+        for r in range(2):
+            product_0(last, r, 2)
+        weave_d1(0, 2)
+        weave_d1(1, 2)
+        weave_d1(0, 3)
+        quant_d1(2)
+        weave_d1(1, 3)
+        for m in range(2):
+            for r in range(2):
+                empty_1(m, r, "S")
+        for m in (2, 3):
+            for r in range(2):
+                product_1(m, r, "acc" if m == 2 else "turn")
+        weave_d1(0, 4)
+        quant_d1(3)
+        weave_d1(1, 4)
         out_0_empty(last)
-        weave("y", 1, 1, "V")
-        quant_e4("y", 0, 1)
+        empty_1(2, 0, "V")
+        quant_d1(4)
+        empty_1(2, 1, "S")
+        empty_1(3, 0, "S")
+        empty_1(3, 1, "V")
         for m in range(4, 8):
-            product_1(m, 0, "turn")
-            empty_1(m, 0, "S")
-        for m in range(4):
-            product_1(m, 1, "acc", 0, 1)
-        quant_e4("y", 1, 1)
-        for m in range(4):
-            product_1(m, 1, "acc", 1)
-            empty_1(m, 1, "VS"[m % 2])
-        for m in range(4, 8):
-            product_1(m, 1, "turn")
-            empty_1(m, 1, "VS"[m % 2])
+            for r in range(2):
+                product_1(m, r, "acc" if m % 2 == 1 else "turn")
+                empty_1(m, r, "SV"[r])

@@ -89,27 +89,30 @@ def tile_instrumentedlocmblock_pb_v_kernel(
         def paired(ap):
             return ap.rearrange("p (w u i) -> p u w i", u=2, i=2)
 
-        def make_d2(c):
-            tiles["d2", c] = work.tile([P, G], F32, name="d2")
+        def make_d2(c, groups=slice(0, 2 * P)):
+            if groups.start == 0:
+                tiles["d2", c] = work.tile([P, G], F32, name="d2")
             nc.vector.tensor_tensor(
-                out=tiles["d2", c][:].rearrange("p (u i w) -> p u w i", u=2, i=2),
-                in0=paired(tiles["gate", c][:]), in1=paired(rows("go", c)), op=ALU.mult)
+                out=tiles["d2", c][:].rearrange("p (u i w) -> p u w i", u=2, i=2)[:, :, groups],
+                in0=paired(tiles["gate", c][:])[:, :, groups], in1=paired(rows("go", c))[:, :, groups], op=ALU.mult)
 
-        def make_slope(c):
-            tiles["slope", c] = work.tile([P, G], F32, name="slope", bufs=1)
+        def make_slope(c, groups=slice(0, 2 * P)):
+            if groups.start == 0:
+                tiles["slope", c] = work.tile([P, G], F32, name="slope", bufs=1)
+            cols = slice(PACK * groups.start, PACK * groups.stop)
             nc.vector.scalar_tensor_tensor(
-                out=tiles["slope", c][:], in0=tiles["gate", c][:], scalar=1.0, in1=rows("v", c),
+                out=tiles["slope", c][:, cols], in0=tiles["gate", c][:, cols], scalar=1.0, in1=rows("v", c)[:, cols],
                 op0=ALU.subtract, op1=ALU.mult)
 
-        def make_d1(c):
+        def make_d1(c, groups=slice(0, 2 * P), us=(0, 1)):
             half, j = divmod(c, PACK)
             if j == 0:
                 tiles["d1", half] = work.tile([P, PACK * G], BF16, name="d1")
-            for u in range(2):
+            for u in us:
                 nc.vector.scalar_tensor_tensor(
-                    out=tiles["d1", half][:, j * G + u * HALF:j * G + (u + 1) * HALF].rearrange("p (w i) -> p w i", i=2),
-                    in0=paired(tiles["slope", c][:])[:, u], scalar=-1.0,
-                    in1=tiles["d2", c][:, u * HALF:(u + 1) * HALF].rearrange("p (i w) -> p w i", i=2),
+                    out=tiles["d1", half][:, j * G + u * HALF:j * G + (u + 1) * HALF].rearrange("p (w i) -> p w i", i=2)[:, groups],
+                    in0=paired(tiles["slope", c][:])[:, u, groups], scalar=-1.0,
+                    in1=tiles["d2", c][:, u * HALF:(u + 1) * HALF].rearrange("p (i w) -> p w i", i=2)[:, groups],
                     op0=ALU.mult, op1=ALU.mult)
 
         def turn_d2(c, g):
@@ -218,7 +221,7 @@ def tile_instrumentedlocmblock_pb_v_kernel(
 
         def empty_0(c, r, eng="S"):
             if r == 0:
-                tiles["res0", c] = work.tile([P, R], F32, name="result", bufs=4)
+                tiles["res0", c] = work.tile([P, R], F32, name="result", bufs=5)
             copiers[eng](out=tiles["res0", c][:, r * HALF:(r + 1) * HALF], in_=tiles["acc0", c, r][:])
             if r == 1:
                 half, j = divmod(c, PACK)
@@ -226,7 +229,7 @@ def tile_instrumentedlocmblock_pb_v_kernel(
 
         def empty_1(m, r, eng):
             if r == 0:
-                tiles["res1", m] = work.tile([P, R], F32, name="result", bufs=4)
+                tiles["res1", m] = work.tile([P, R], F32, name="result", bufs=5)
             res = tiles["res1", m]
             copiers[eng](out=res[:, r * HALF:(r + 1) * HALF], in_=tiles["acc1", m, r][:])
             if r == 1:
@@ -268,11 +271,11 @@ def tile_instrumentedlocmblock_pb_v_kernel(
         load_raw("w1", glu_w1, 0)
         load_rows("v", value, F32, 0, 1)
         nc.gpsimd.memset(dt_raw[:], 0.0)
-        nc.scalar.dma_start(out=dt_raw[0:1, :], in_=dt.unsqueeze(0))
         nc.scalar.activation(out=warm[:], in_=ident[:, 0:1], func=ACT.Sigmoid)
         load_rows("x", gate_pre, F32, 1, 1)
         load_rows("go", grad_out, BF16, 1, 1)
         load_rows("v", value, F32, 1, 1)
+        nc.sync.dma_start(out=dt_raw[0:1, :], in_=dt.unsqueeze(0))
         load_rows("x", gate_pre, F32, 2, 1)
         load_raw("w2", glu_w2, 0)
         load_rows("go", grad_out, BF16, 2, 2)
@@ -280,25 +283,25 @@ def tile_instrumentedlocmblock_pb_v_kernel(
         load_rows("x", gate_pre, F32, 3, 1)
         load_raw("w1", glu_w1, 1)
         load_rows("v", value, F32, 3, 1)
-        load_rows("x", gate_pre, F32, 4, 2)
+        load_rows("x", gate_pre, F32, 4, 1)
         load_raw("w2", glu_w2, 1)
-        load_rows("go", grad_out, BF16, 4, 2)
+        load_rows("go", grad_out, BF16, 4, 1)
         load_rows("v", value, F32, 4, 1)
         load_raw("y", y_tilde, 0)
         pre = {
             0: [W("w1", 0, 1, "S")],
-            1: [take_dt],
-            3: [W("w1", 1, 1, "S")],
+            3: [W("w1", 1, 0, "S")],
+            4: [W("w2", 1, 1, "S")],
             5: [WY(0, 0)],
             7: [WY(1, 1)],
         }
         post = {
-            1: [W("w2", 0, 0, "S")],
-            2: [W("w2", 0, 1, "S"), L("y", y_tilde, 1), W("w1", 1, 0, "S")],
-            3: [W("w2", 1, 1, "S")],
-            4: [H(0, 0), H(1, 0), H(0, 1), H(1, 1)],
-            5: [H(2, 0), H(2, 1), WY(0, 1), H(3, 0), H(3, 1)],
-            6: [WY(1, 0), H(4, 0), H(4, 1), WD(0, 0, "S"), WD(0, 1, "S")],
+            1: [spread_dt, W("w2", 0, 0, "S"), take_dt],
+            2: [W("w2", 0, 1, "S"), L("y", y_tilde, 1)],
+            3: [W("w1", 1, 1, "S"), L("z", z_next, 1), LR("go", grad_out, BF16, 6, 2), LR("v", value, F32, 6, 2)],
+            4: [H(0, 0), H(1, 0), H(2, 0)],
+            5: [H(0, 1), H(1, 1), WY(0, 1), H(2, 1), H(3, 0)],
+            6: [WY(1, 0), H(3, 1), H(4, 0), H(4, 1)],
             7: [H(5, 0), H(5, 1)],
         }
         between = {
@@ -309,30 +312,29 @@ def tile_instrumentedlocmblock_pb_v_kernel(
             0: [Q("w1", 0, 0)],
             2: [Q("w2", 0, 0)],
             3: [Q("w2", 0, 1)],
-            4: [Q("w2", 1, 1), Y(0, 0, 0)],
+            4: [Q("w1", 1, 1)],
             5: [Y(0, 1, 1)],
             6: [Q("y", 0, 1)],
             7: [Q("y", 1, 1)],
         }
         end = {
-            0: [Q("w1", 0, 1), spread_dt, L("z", z_next, 0), LR("v", value, F32, 5, 1)],
+            0: [Q("w1", 0, 1), L("z", z_next, 0), LR("x", gate_pre, F32, 5, 1), LR("go", grad_out, BF16, 5, 1), LR("v", value, F32, 5, 1)],
             1: [LR("x", gate_pre, F32, 6, 2)],
-            3: [Q("w1", 1, 0), W("w2", 1, 0, "V"), Q("w1", 1, 1), L("z", z_next, 1), LR("go", grad_out, BF16, 6, 2), LR("v", value, F32, 6, 2), Q("w2", 1, 0)],
-            4: [Y(0, 0, 1), Y(0, 1, 0)],
+            3: [W("w2", 1, 0, "V"), Q("w1", 1, 0), Q("w2", 1, 0)],
+            4: [Y(0, 0, 0), Y(0, 0, 1), Q("w2", 1, 1), Y(0, 1, 0)],
             5: [Q("y", 0, 0), Y(1, 0, 0), Y(1, 0, 1)],
             6: [Y(1, 1, 0), Y(1, 1, 1), Q("y", 1, 0)],
         }
         sigmoid(0)
-        for c in range(CHUNKS):
+        last = CHUNKS - 1
+        for c in range(last):
             if c > 0:
                 turn_d1(c - 1)
-                if c < 7:
-                    empty_d2(c - 1, 0)
-                    empty_d2(c - 1, 1)
+                empty_d2(c - 1, 0)
+                empty_d2(c - 1, 1)
                 empty_d1(c - 1)
             run(pre.get(c, []))
-            if c + 1 < CHUNKS:
-                sigmoid(c + 1)
+            sigmoid(c + 1)
             make_d2(c)
             run(between.get(c, []))
             make_slope(c)
@@ -340,52 +342,76 @@ def tile_instrumentedlocmblock_pb_v_kernel(
             run(post.get(c, []))
             turn_d2(c, 0)
             turn_d2(c, 1)
-            if c >= 6:
+            if c == 6:
                 empty_d2(c, 0)
                 empty_d2(c, 1)
-            if c == 7:
-                out_0_tile(6)
             make_d1(c)
-            if 0 < c < 7:
+            if c > 0:
                 quant_feature(c - 1)
             run(end.get(c, []))
-        last = CHUNKS - 1
-        turn_d1(last)
-        out_0_empty(last - 1)
-        quant_feature(last, 1, 1)
-        empty_d1(last)
+        turn_d1(6)
+        empty_d1(6)
+        out_0_tile(5)
+        quant_feature(6)
+        out_0_tile(6)
+        weave_d1(0, 0, "S")
+        weave_d1(0, 1, "S")
+        weave_y(1, 1, "S")
+        make_d2(last)
+        quant_d1(0, 0, 1)
+        quant_d1(1, 0, 1)
+        turn_d2(last, 0)
+        turn_d2(last, 1)
+        make_slope(last)
+        out_0_empty(5)
+        for m in range(2):
+            for r in range(2):
+                product_1(m, r, "turn" if m == 0 else "acc", 0, 1)
+        empty_d2(last, 0)
+        empty_d2(last, 1)
+        quant_e4("y", 1, 1)
+        head, rest = slice(0, 64), slice(64, 2 * P)
+        make_d1(last, head)
+        make_d1(last, rest, (0,))
         weave_d1(1, 0)
         weave_d1(1, 1)
+        quant_d1(0, 1, 1)
+        make_d1(last, rest, (1,))
+        quant_d1(1, 1, 1)
+        quant_feature(last, 1, 1)
+        out_0_empty(6)
+        for m in range(2):
+            for r in range(2):
+                product_1(m, r, "", 1)
+        turn_d1(last)
         for r in range(2):
             product_0(last, r, 0, 2)
-        quant_d1(0)
-        quant_d1(1)
-        for m in range(2):
-            for r in range(2):
-                product_1(m, r, "turn")
-        quant_feature(last, 0, 1)
-        for r in range(2):
-            product_0(last, r, 2)
         weave_d1(0, 2)
         weave_d1(1, 2)
-        weave_d1(0, 3)
+        empty_1(0, 0, "S")
+        empty_1(0, 1, "S")
+        empty_d1(last)
         quant_d1(2)
+        empty_1(1, 0, "S")
+        empty_1(1, 1, "S")
+        quant_feature(last, 0, 1)
+        for r in range(2):
+            product_1(2, r, "turn")
+        for r in range(2):
+            product_0(last, r, 2)
+        for r in range(2):
+            product_1(3, r, "acc")
+        weave_d1(0, 3)
         weave_d1(1, 3)
-        for m in range(2):
-            for r in range(2):
-                empty_1(m, r, "S")
-        for m in (2, 3):
-            for r in range(2):
-                product_1(m, r, "acc" if m == 2 else "turn")
+        for r in range(2):
+            empty_1(2, r, "S")
         weave_d1(0, 4)
         quant_d1(3)
-        weave_d1(1, 4)
         out_0_empty(last)
-        empty_1(2, 0, "V")
+        weave_d1(1, 4)
+        empty_1(3, 0, "V")
         quant_d1(4)
-        empty_1(2, 1, "S")
-        empty_1(3, 0, "S")
-        empty_1(3, 1, "V")
+        empty_1(3, 1, "S")
         for m in range(4, 8):
             for r in range(2):
                 product_1(m, r, "acc" if m % 2 == 1 else "turn")

@@ -20,8 +20,8 @@ P = 128
 PACK = 4
 HALF = 512
 CHUNKS = 8
-PARTS = [(0, 1), (1, 1), (2, 2), (4, 2), (6, 2)]
-PART_OF = [0, 1, 2, 2, 3, 3, 4, 4]
+PARTS = [(0, 1), (1, 1), (2, 1), (3, 1), (4, 2), (6, 2)]
+PART_OF = [0, 1, 2, 3, 4, 4, 5, 5]
 
 
 def tile_instrumentedlocmblock_pb_v_kernel(
@@ -40,7 +40,6 @@ def tile_instrumentedlocmblock_pb_v_kernel(
         dt_raw = keep.tile([P, 1], BF16, name="dt_raw")
         dt_first = keep.tile([P, 1], F32, name="dt_first")
         dt_col = keep.tile([P, 1], F32, name="dt_col")
-        warm = keep.tile([P, 1], F32, name="warm")
 
         copiers = {"V": nc.vector.tensor_copy, "S": nc.scalar.copy}
         tiles = {}
@@ -57,6 +56,11 @@ def tile_instrumentedlocmblock_pb_v_kernel(
                 out=tiles[name, pair][:, (c % 2) * G:(c % 2 + count) * G],
                 in_=token_rows(tensor, c // PACK)[:, j * G:(j + count) * G],
             )
+
+        def load_first_x(cols):
+            if cols.start == 0:
+                tiles["x", 0] = load.tile([P, 2 * G], F32, name="x")
+            nc.sync.dma_start(out=tiles["x", 0][:, cols], in_=token_rows(gate_pre, 0)[:, cols])
 
         def rows(name, c):
             return tiles[name, c // 2][:, (c % 2) * G:(c % 2 + 1) * G]
@@ -82,9 +86,10 @@ def tile_instrumentedlocmblock_pb_v_kernel(
         def take_dt():
             nc.scalar.copy(out=dt_col[:], in_=tiles["dt_bank"][:, 0:1])
 
-        def sigmoid(c):
-            tiles["gate", c] = work.tile([P, G], F32, name="gate")
-            nc.scalar.activation(out=tiles["gate", c][:], in_=rows("x", c), func=ACT.Sigmoid)
+        def sigmoid(c, cols=slice(0, G)):
+            if cols.start == 0:
+                tiles["gate", c] = work.tile([P, G], F32, name="gate")
+            nc.scalar.activation(out=tiles["gate", c][:, cols], in_=rows("x", c)[:, cols], func=ACT.Sigmoid)
 
         def paired(ap):
             return ap.rearrange("p (w u i) -> p u w i", u=2, i=2)
@@ -246,8 +251,7 @@ def tile_instrumentedlocmblock_pb_v_kernel(
 
         def load_chunks(c, count):
             load_rows("x", gate_pre, F32, c, count)
-            if c % 2 == 0:
-                load_rows("go", grad_out, BF16, c, 2)
+            load_rows("go", grad_out, BF16, c, count)
             load_rows("v", value, F32, c, count)
         W = lambda name, g, r, eng: (lambda: weave(name, g, r, eng))
         Q = lambda name, g, r: (lambda: quant_e4(name, g, r))
@@ -266,37 +270,35 @@ def tile_instrumentedlocmblock_pb_v_kernel(
         WY = lambda h, r: (lambda: weave_y(h, r, "S"))
         LR = lambda name, t, d, c, n: (lambda: load_rows(name, t, d, c, n))
 
-        load_rows("x", gate_pre, F32, 0, 1)
+        load_first_x(slice(0, HALF))
         load_rows("go", grad_out, BF16, 0, 1)
-        load_raw("w1", glu_w1, 0)
+        load_first_x(slice(HALF, G))
         load_rows("v", value, F32, 0, 1)
-        nc.gpsimd.memset(dt_raw[:], 0.0)
-        nc.scalar.activation(out=warm[:], in_=ident[:, 0:1], func=ACT.Sigmoid)
         load_rows("x", gate_pre, F32, 1, 1)
+        load_raw("w1", glu_w1, 0)
+        nc.gpsimd.memset(dt_raw[:], 0.0)
         load_rows("go", grad_out, BF16, 1, 1)
         load_rows("v", value, F32, 1, 1)
         nc.sync.dma_start(out=dt_raw[0:1, :], in_=dt.unsqueeze(0))
         load_rows("x", gate_pre, F32, 2, 1)
         load_raw("w2", glu_w2, 0)
-        load_rows("go", grad_out, BF16, 2, 2)
+        load_rows("go", grad_out, BF16, 2, 1)
         load_rows("v", value, F32, 2, 1)
-        load_rows("x", gate_pre, F32, 3, 1)
+        load_chunks(3, 1)
         load_raw("w1", glu_w1, 1)
-        load_rows("v", value, F32, 3, 1)
         load_rows("x", gate_pre, F32, 4, 1)
         load_raw("w2", glu_w2, 1)
         load_rows("go", grad_out, BF16, 4, 1)
         load_rows("v", value, F32, 4, 1)
         load_raw("y", y_tilde, 0)
         pre = {
-            0: [W("w1", 0, 1, "S")],
             3: [W("w1", 1, 0, "S")],
             4: [W("w2", 1, 1, "S")],
             5: [WY(0, 0)],
             7: [WY(1, 1)],
         }
         post = {
-            1: [spread_dt, W("w2", 0, 0, "S"), take_dt],
+
             2: [W("w2", 0, 1, "S"), L("y", y_tilde, 1)],
             3: [W("w1", 1, 1, "S"), L("z", z_next, 1), LR("go", grad_out, BF16, 6, 2), LR("v", value, F32, 6, 2)],
             4: [H(0, 0), H(1, 0), H(2, 0)],
@@ -305,11 +307,10 @@ def tile_instrumentedlocmblock_pb_v_kernel(
             7: [H(5, 0), H(5, 1)],
         }
         between = {
-            0: [W("w1", 0, 0, "V")],
             7: [lambda: quant_feature(6)],
         }
         spacer = {
-            0: [Q("w1", 0, 0)],
+            1: [Q("w1", 0, 0)],
             2: [Q("w2", 0, 0)],
             3: [Q("w2", 0, 1)],
             4: [Q("w1", 1, 1)],
@@ -318,31 +319,37 @@ def tile_instrumentedlocmblock_pb_v_kernel(
             7: [Q("y", 1, 1)],
         }
         end = {
-            0: [Q("w1", 0, 1), L("z", z_next, 0), LR("x", gate_pre, F32, 5, 1), LR("go", grad_out, BF16, 5, 1), LR("v", value, F32, 5, 1)],
-            1: [LR("x", gate_pre, F32, 6, 2)],
+            0: [W("w1", 0, 0, "V"), W("w1", 0, 1, "S"), L("z", z_next, 0), LR("x", gate_pre, F32, 5, 1), LR("go", grad_out, BF16, 5, 1), LR("v", value, F32, 5, 1)],
+            1: [Q("w1", 0, 1), LR("x", gate_pre, F32, 6, 2), spread_dt, W("w2", 0, 0, "S"), take_dt],
             3: [W("w2", 1, 0, "V"), Q("w1", 1, 0), Q("w2", 1, 0)],
             4: [Y(0, 0, 0), Y(0, 0, 1), Q("w2", 1, 1), Y(0, 1, 0)],
             5: [Q("y", 0, 0), Y(1, 0, 0), Y(1, 0, 1)],
             6: [Y(1, 1, 0), Y(1, 1, 1), Q("y", 1, 0)],
         }
-        sigmoid(0)
+        sigmoid(0, slice(0, HALF))
+        sigmoid(0, slice(HALF, G))
         last = CHUNKS - 1
         for c in range(last):
             if c > 0:
                 turn_d1(c - 1)
-                empty_d2(c - 1, 0)
-                empty_d2(c - 1, 1)
+                if c > 2:
+                    empty_d2(c - 1, 0)
+                    empty_d2(c - 1, 1)
                 empty_d1(c - 1)
             run(pre.get(c, []))
             sigmoid(c + 1)
-            make_d2(c)
+            if c == 0:
+                make_d2(c, slice(0, P))
+                make_d2(c, slice(P, 2 * P))
+            else:
+                make_d2(c)
             run(between.get(c, []))
             make_slope(c)
             run(spacer.get(c, []))
             run(post.get(c, []))
             turn_d2(c, 0)
             turn_d2(c, 1)
-            if c == 6:
+            if c in (0, 1, 6):
                 empty_d2(c, 0)
                 empty_d2(c, 1)
             make_d1(c)
@@ -384,35 +391,48 @@ def tile_instrumentedlocmblock_pb_v_kernel(
             for r in range(2):
                 product_1(m, r, "", 1)
         turn_d1(last)
-        for r in range(2):
-            product_0(last, r, 0, 2)
+        product_0(last, 0, 0, 2)
         weave_d1(0, 2)
         weave_d1(1, 2)
-        empty_1(0, 0, "S")
-        empty_1(0, 1, "S")
-        empty_d1(last)
+        weave_d1(0, 3)
         quant_d1(2)
-        empty_1(1, 0, "S")
-        empty_1(1, 1, "S")
-        quant_feature(last, 0, 1)
+        weave_d1(1, 3)
+        for m in range(2):
+            for r in range(2):
+                empty_1(m, r, "S")
+        empty_d1(last)
         for r in range(2):
             product_1(2, r, "turn")
-        for r in range(2):
-            product_0(last, r, 2)
-        for r in range(2):
-            product_1(3, r, "acc")
-        weave_d1(0, 3)
-        weave_d1(1, 3)
-        for r in range(2):
-            empty_1(2, r, "S")
+        product_0(last, 1, 0, 2)
         weave_d1(0, 4)
         quant_d1(3)
-        out_0_empty(last)
+        for r in range(2):
+            product_1(3, r, "acc")
         weave_d1(1, 4)
-        empty_1(3, 0, "V")
+        for r in range(2):
+            empty_1(2, r, "S")
+        weave_d1(0, 5)
         quant_d1(4)
-        empty_1(3, 1, "S")
-        for m in range(4, 8):
+        for r in range(2):
+            product_1(4, r, "turn")
+        for r in range(2):
+            empty_1(3, r, "S")
+        for r in range(2):
+            product_1(5, r, "turn")
+        weave_d1(1, 5)
+        quant_feature(last, 0, 1)
+        quant_d1(5)
+        for r in range(2):
+            product_0(last, r, 2)
+        for m in (4, 5):
             for r in range(2):
-                product_1(m, r, "acc" if m % 2 == 1 else "turn")
+                empty_1(m, r, "SV"[r])
+        for r in range(2):
+            product_1(6, r, "turn")
+        empty_0(last, 0, "S")
+        empty_0(last, 1, "V")
+        for r in range(2):
+            product_1(7, r, "acc")
+        for m in (6, 7):
+            for r in range(2):
                 empty_1(m, r, "SV"[r])

@@ -286,8 +286,8 @@ def tile_instrumentedlocmblock_pb_v_kernel(
         load_rows("v", value, F32, 2, 1)
         load_chunks(3, 1)
         load_raw("w1", glu_w1, 1)
-        load_rows("x", gate_pre, F32, 4, 1)
         load_raw("w2", glu_w2, 1)
+        load_rows("x", gate_pre, F32, 4, 1)
         load_rows("go", grad_out, BF16, 4, 1)
         load_rows("v", value, F32, 4, 1)
         load_raw("y", y_tilde, 0)
@@ -300,10 +300,10 @@ def tile_instrumentedlocmblock_pb_v_kernel(
         post = {
 
             2: [W("w2", 0, 1, "S"), L("y", y_tilde, 1)],
-            3: [W("w1", 1, 1, "S"), L("z", z_next, 1), LR("go", grad_out, BF16, 6, 2), LR("v", value, F32, 6, 2)],
+            3: [W("w1", 1, 1, "S")],
             4: [H(0, 0), H(1, 0), H(2, 0)],
             5: [H(0, 1), H(1, 1), WY(0, 1), H(2, 1), H(3, 0)],
-            6: [WY(1, 0), H(3, 1), H(4, 0), H(4, 1)],
+            6: [H(3, 1), H(4, 0), H(4, 1)],
             7: [H(5, 0), H(5, 1)],
         }
         between = {
@@ -320,11 +320,11 @@ def tile_instrumentedlocmblock_pb_v_kernel(
         }
         end = {
             0: [W("w1", 0, 0, "V"), W("w1", 0, 1, "S"), L("z", z_next, 0), LR("x", gate_pre, F32, 5, 1), LR("go", grad_out, BF16, 5, 1), LR("v", value, F32, 5, 1)],
-            1: [Q("w1", 0, 1), LR("x", gate_pre, F32, 6, 2), spread_dt, W("w2", 0, 0, "S"), take_dt],
-            3: [W("w2", 1, 0, "V"), Q("w1", 1, 0), Q("w2", 1, 0)],
+            1: [Q("w1", 0, 1), LR("x", gate_pre, F32, 6, 2), LR("go", grad_out, BF16, 6, 2), LR("v", value, F32, 6, 1), spread_dt, W("w2", 0, 0, "S"), take_dt],
+            3: [W("w2", 1, 0, "V"), Q("w1", 1, 0), L("z", z_next, 1), LR("v", value, F32, 7, 1), Q("w2", 1, 0)],
             4: [Y(0, 0, 0), Y(0, 0, 1), Q("w2", 1, 1), Y(0, 1, 0)],
-            5: [Q("y", 0, 0), Y(1, 0, 0), Y(1, 0, 1)],
-            6: [Y(1, 1, 0), Y(1, 1, 1), Q("y", 1, 0)],
+            5: [Q("y", 0, 0)],
+            6: [Y(1, 0, 0), Y(1, 0, 1), Y(1, 1, 0), Y(1, 1, 1)],
         }
         sigmoid(0, slice(0, HALF))
         sigmoid(0, slice(HALF, G))
@@ -363,10 +363,12 @@ def tile_instrumentedlocmblock_pb_v_kernel(
         out_0_tile(6)
         weave_d1(0, 0, "S")
         weave_d1(0, 1, "S")
+        weave_y(1, 0, "S")
         weave_y(1, 1, "S")
         make_d2(last)
         quant_d1(0, 0, 1)
         quant_d1(1, 0, 1)
+        quant_e4("y", 1, 0)
         turn_d2(last, 0)
         turn_d2(last, 1)
         make_slope(last)

from contextlib import ExitStack

import concourse.mybir as mybir
from concourse.masks import make_identity

B, R, G = 1024, 1024, 1024
FLOPS = 3 * 2 * B * R * G
BYTES = 5 * B * G * 2 + 2 * B * G * 4 + 2 * B * R * 4 + 2

F32 = mybir.dt.float32
BF16 = mybir.dt.bfloat16
U32 = mybir.dt.uint32
U8 = mybir.dt.uint8
E4X4 = mybir.dt.float8_e4m3fn_x4
E5X4 = mybir.dt.float8_e5m2_x4
ALU = mybir.AluOpType
ACT = mybir.ActivationFunctionType

P = 128
PACK = 4
HALF = 512
CHUNKS = 8
PARTS = [(0, 1), (1, 1), (2, 1), (3, 1), (4, 2), (6, 2)]
PART_OF = [0, 1, 2, 3, 4, 4, 5, 5]


def tile_instrumentedlocmblock_pb_v_kernel(
    tc, y_tilde, z_next, dt, glu_w1, glu_w2, glu_b1, glu_b2, gate_pre, value, grad_out, out_0, out_1
):
    nc = tc.nc
    with ExitStack() as ctx:
        keep = ctx.enter_context(tc.tile_pool(name="keep", bufs=1))
        load = ctx.enter_context(tc.tile_pool(name="load", bufs=3))
        work = ctx.enter_context(tc.tile_pool(name="work", bufs=2))
        psum = ctx.enter_context(tc.psum_pool(name="psum", bufs=4))
        ctx.enter_context(tc.manual_schedule())

        ident = keep.tile([P, P], F32, name="ident")
        make_identity(nc, ident[:])
        dt_raw = keep.tile([P, 1], BF16, name="dt_raw")
        dt_first = keep.tile([P, 1], F32, name="dt_first")
        dt_col = keep.tile([P, 1], F32, name="dt_col")

        copiers = {"V": nc.vector.tensor_copy, "S": nc.scalar.copy}
        tiles = {}

        def token_rows(tensor, half):
            return tensor[half * HALF:(half + 1) * HALF, :].rearrange("(p j) w -> p (j w)", j=PACK)

        def load_rows(name, tensor, dtype, c, count):
            pair = c // 2
            if (name, pair) not in tiles:
                tiles[name, pair] = load.tile([P, 2 * G], dtype, name=name)
            j = c % PACK
            nc.sync.dma_start(
                out=tiles[name, pair][:, (c % 2) * G:(c % 2 + count) * G],
                in_=token_rows(tensor, c // PACK)[:, j * G:(j + count) * G],
            )

        def load_first_x(cols):
            if cols.start == 0:
                tiles["x", 0] = load.tile([P, 2 * G], F32, name="x")
            nc.sync.dma_start(out=tiles["x", 0][:, cols], in_=token_rows(gate_pre, 0)[:, cols])

        def rows(name, c):
            return tiles[name, c // 2][:, (c % 2) * G:(c % 2 + 1) * G]

        def load_raw(name, tensor, half):
            tiles[name, half] = load.tile([P, PACK * R], BF16, name="raw", bufs=5)
            nc.sync.dma_start(out=tiles[name, half][:], in_=token_rows(tensor, half))

        def raw_cols(name, half, r):
            return tiles[name, half][:].rearrange("p (j w) -> p j w", j=PACK)[:, :, r * HALF:(r + 1) * HALF]

        def new_mx(key, width, pool, tag, bufs):
            codes = pool.tile([P, width], U32, name=tag + "_codes", bufs=bufs, align_bytes=64)
            scales = pool.tile([P, width], U8, name=tag + "_scales", bufs=bufs, align_bytes=64)
            tiles[key] = (codes, scales)

        def spread_dt():
            nc.scalar.copy(out=dt_first[:], in_=dt_raw[:])
            bank = psum.tile([P, HALF], F32, name="acc")
            nc.tensor.transpose(bank[:, 0:P], dt_first[:].to_broadcast([P, P]), ident[:])
            tiles["dt_bank"] = bank

        def take_dt():
            nc.scalar.copy(out=dt_col[:], in_=tiles["dt_bank"][:, 0:1])

        def sigmoid(c, cols=slice(0, G)):
            if cols.start == 0:
                tiles["gate", c] = work.tile([P, G], F32, name="gate")
            nc.scalar.activation(out=tiles["gate", c][:, cols], in_=rows("x", c)[:, cols], func=ACT.Sigmoid)

        def paired(ap):
            return ap.rearrange("p (w u i) -> p u w i", u=2, i=2)

        def make_d2(c, groups=slice(0, 2 * P)):
            if groups.start == 0:
                tiles["d2", c] = work.tile([P, G], F32, name="d2")
            nc.vector.tensor_tensor(
                out=tiles["d2", c][:].rearrange("p (u i w) -> p u w i", u=2, i=2)[:, :, groups],
                in0=paired(tiles["gate", c][:])[:, :, groups], in1=paired(rows("go", c))[:, :, groups], op=ALU.mult)

        def make_slope(c, groups=slice(0, 2 * P)):
            if groups.start == 0:
                tiles["slope", c] = work.tile([P, G], F32, name="slope", bufs=1)
            cols = slice(PACK * groups.start, PACK * groups.stop)
            nc.vector.scalar_tensor_tensor(
                out=tiles["slope", c][:, cols], in0=tiles["gate", c][:, cols], scalar=1.0, in1=rows("v", c)[:, cols],
                op0=ALU.subtract, op1=ALU.mult)

        def make_d1(c, groups=slice(0, 2 * P), us=(0, 1)):
            half, j = divmod(c, PACK)
            if j == 0:
                tiles["d1", half] = work.tile([P, PACK * G], BF16, name="d1")
            for u in us:
                nc.vector.scalar_tensor_tensor(
                    out=tiles["d1", half][:, j * G + u * HALF:j * G + (u + 1) * HALF].rearrange("p (w i) -> p w i", i=2)[:, groups],
                    in0=paired(tiles["slope", c][:])[:, u, groups], scalar=-1.0,
                    in1=tiles["d2", c][:, u * HALF:(u + 1) * HALF].rearrange("p (i w) -> p w i", i=2)[:, groups],
                    op0=ALU.mult, op1=ALU.mult)

        def turn_d2(c, g):
            bank = psum.tile([P, HALF], F32, name="turn")
            tiles["turn2", c, g] = bank
            for t in range(PACK):
                first = (2 * t + g) * P
                nc.tensor.transpose(bank[:, t * P:(t + 1) * P], tiles["d2", c][:, first:first + P], ident[:])

        def turn_d1(c):
            half, j = divmod(c, PACK)
            bank = psum.tile([P, HALF], F32, name="turn")
            tiles["turn1", c] = bank
            words = tiles["d1", half][:, j * G:(j + 1) * G].bitcast(F32)
            for g in range(2):
                for u in range(2):
                    nc.tensor.transpose(bank[:, (2 * g + u) * P:(2 * g + u + 1) * P],
                                        words[:, (2 * u + g) * P:(2 * u + g + 1) * P], ident[:])

        def turned(c):
            if ("turned", c) not in tiles:
                tiles["turned", c] = work.tile([P, 2 * G], BF16, name="turned", align_bytes=64)
            return tiles["turned", c]

        def empty_d2(c, g, eng="S"):
            copiers[eng](
                out=turned(c)[:, G + g * HALF:G + (g + 1) * HALF].rearrange("p (n t) -> p n t", t=PACK),
                in_=tiles["turn2", c, g][:].rearrange("p (t n) -> p n t", t=PACK))

        def empty_d1(c, eng="S"):
            copiers[eng](
                out=turned(c)[:, 0:G].bitcast(F32).rearrange("p (g n u) -> p g n u", g=2, u=2),
                in_=tiles["turn1", c][:].rearrange("p (g u n) -> p g n u", g=2, u=2))

        def quantise(key, cols, fmt, source):
            codes, scales = tiles[key]
            nc.vector.quantize_mx(out=codes[:, cols].bitcast(fmt), scales=scales[:, cols], in_=source)

        def quant_feature(c, first=0, count=2):
            if ("dT", c) not in tiles:
                new_mx(("dT", c), HALF, work, "dT", 4)
            quantise(("dT", c), slice(first * 256, (first + count) * 256), E5X4, turned(c)[:, first * G:(first + count) * G])

        def weave(name, half, r, eng):
            woven = work.tile([P, PACK * HALF], BF16, name="woven", bufs=4, align_bytes=64)
            tiles["woven", name, half, r] = woven
            copiers[eng](
                out=woven[:].rearrange("p (c i j) -> p c j i", i=4, j=PACK),
                in_=raw_cols(name, half, r).rearrange("p j (c i) -> p c j i", i=4))

        def quant_e4(name, half, r):
            new_mx((name, half, r), HALF, keep, "%s_%d_%d" % (name, half, r), 1)
            quantise((name, half, r), slice(0, HALF), E4X4, tiles["woven", name, half, r][:])

        def make_y(half, r, h):
            if h == 0:
                tiles["y_pairs", half, r] = work.tile([P, PACK * HALF], BF16, name="y_pairs", bufs=2)
            pairs = tiles["y_pairs", half, r]
            if True:
                nc.vector.scalar_tensor_tensor(
                    out=pairs[:, h * G:(h + 1) * G].rearrange("p (c e) -> p c e", e=2),
                    in0=raw_cols("z", half, r)[:, 2 * h:2 * h + 2, :].rearrange("p e c -> p c e"), scalar=dt_col[:],
                    in1=raw_cols("y", half, r)[:, 2 * h:2 * h + 2, :].rearrange("p e c -> p c e"),
                    op0=ALU.mult, op1=ALU.add)

        def weave_y(half, r, eng):
            woven = work.tile([P, PACK * HALF], BF16, name="woven", bufs=4, align_bytes=64)
            tiles["woven", "y", half, r] = woven
            copiers[eng](
                out=woven[:].bitcast(F32).rearrange("p (c h) -> p c h", h=2),
                in_=tiles["y_pairs", half, r][:].bitcast(F32).rearrange("p (h c) -> p c h", h=2))

        def weave_d1(half, part, eng="V"):
            first, count = PARTS[part]
            if ("woven", "d1", part) not in tiles:
                tiles["woven", "d1", part] = work.tile([P, PACK * HALF], BF16, name="woven", bufs=4, align_bytes=64)
            width = count * HALF
            copiers[eng](
                out=tiles["woven", "d1", part][:, half * width:(half + 1) * width].rearrange("p (w u i j) -> p u w j i", u=2, i=2, j=PACK),
                in_=tiles["d1", half][:].rearrange("p (j u w i) -> p u w j i", j=PACK, u=2, i=2)[:, :, first * 32:(first + count) * 32])

        def quant_d1(part, half=0, halves=2):
            if ("d1q", part) not in tiles:
                new_mx(("d1q", part), HALF, work, "d1q", 3)
            count = PARTS[part][1]
            quantise(("d1q", part), slice(half * count * P, (half + halves) * count * P), E5X4,
                     tiles["woven", "d1", part][:, half * count * HALF:(half + halves) * count * HALF])

        def product(key, passes, tag="acc", first=0, stop=None):
            if first == 0:
                tiles[key] = psum.tile([P, HALF], F32, name=tag)
            acc = tiles[key]
            for n, (left, block, right) in list(enumerate(passes))[first:stop]:
                cols = slice(block * P, (block + 1) * P)
                nc.tensor.matmul_mx(
                    out=acc[:], lhsT=tiles[left][0][:, cols].bitcast(E5X4), lhsT_scale=tiles[left][1][:, cols],
                    rhs=tiles[right][0][:].bitcast(E4X4), rhs_scale=tiles[right][1][:],
                    start=(n == 0), stop=(n == len(passes) - 1))

        def product_0(c, r, first=0, stop=None):
            product(("acc0", c, r), [(("dT", c), 2 * m + g, (name, g, r))
                                     for m, name in ((1, "w2"), (0, "w1")) for g in range(2)], "acc", first, stop)

        def product_1(m, r, tag="acc", first=0, stop=None):
            product(("acc1", m, r), [(("d1q", PART_OF[m]), PARTS[PART_OF[m]][1] * half + m - PARTS[PART_OF[m]][0], ("y", half, r)) for half in range(2)], tag, first, stop)

        def empty_0(c, r, eng="S"):
            if r == 0:
                tiles["res0", c] = work.tile([P, R], F32, name="result", bufs=5)
            copiers[eng](out=tiles["res0", c][:, r * HALF:(r + 1) * HALF], in_=tiles["acc0", c, r][:])
            if r == 1:
                half, j = divmod(c, PACK)
                nc.sync.dma_start(out=token_rows(out_0, half)[:, j * R:(j + 1) * R], in_=tiles["res0", c][:])

        def empty_1(m, r, eng):
            if r == 0:
                tiles["res1", m] = work.tile([P, R], F32, name="result", bufs=5)
            res = tiles["res1", m]
            copiers[eng](out=res[:, r * HALF:(r + 1) * HALF], in_=tiles["acc1", m, r][:])
            if r == 1:
                nc.sync.dma_start(out=out_1[m * P:(m + 1) * P, :], in_=res[:])

        def out_0_tile(c):
            for r in range(2):
                product_0(c, r)

        def out_0_empty(c):
            for r in range(2):
                empty_0(c, r)


        def load_chunks(c, count):
            load_rows("x", gate_pre, F32, c, count)
            load_rows("go", grad_out, BF16, c, count)
            load_rows("v", value, F32, c, count)
        W = lambda name, g, r, eng: (lambda: weave(name, g, r, eng))
        Q = lambda name, g, r: (lambda: quant_e4(name, g, r))
        L = lambda name, t, h: (lambda: load_raw(name, t, h))
        LC = lambda c, n: (lambda: load_chunks(c, n))
        Y = lambda t, r, h: (lambda: make_y(t, r, h))
        WD = lambda h, g, eng="V": (lambda: weave_d1(h, g, eng))
        QD = lambda g: (lambda: quant_d1(g))
        M0 = lambda c: (lambda: out_0_tile(c))
        E0 = lambda c: (lambda: out_0_empty(c))
        def run(steps):
            for step in steps:
                step()

        H = lambda c, r, eng="S": (lambda: (product_0(c, r), empty_0(c, r, eng)))
        WY = lambda h, r: (lambda: weave_y(h, r, "S"))
        LR = lambda name, t, d, c, n: (lambda: load_rows(name, t, d, c, n))

        load_first_x(slice(0, HALF))
        load_rows("go", grad_out, BF16, 0, 1)
        load_first_x(slice(HALF, G))
        load_rows("v", value, F32, 0, 1)
        load_rows("x", gate_pre, F32, 1, 1)
        load_raw("w1", glu_w1, 0)
        nc.gpsimd.memset(dt_raw[:], 0.0)
        load_rows("go", grad_out, BF16, 1, 1)
        load_rows("v", value, F32, 1, 1)
        nc.sync.dma_start(out=dt_raw[0:1, :], in_=dt.unsqueeze(0))
        load_rows("x", gate_pre, F32, 2, 1)
        load_raw("w2", glu_w2, 0)
        load_rows("go", grad_out, BF16, 2, 1)
        load_rows("v", value, F32, 2, 1)
        load_chunks(3, 1)
        load_raw("w1", glu_w1, 1)
        load_raw("w2", glu_w2, 1)
        load_rows("x", gate_pre, F32, 4, 1)
        load_rows("go", grad_out, BF16, 4, 1)
        load_rows("v", value, F32, 4, 1)
        load_raw("y", y_tilde, 0)
        pre = {
            3: [W("w1", 1, 0, "S")],
            4: [W("w2", 1, 1, "S")],
            5: [WY(0, 0)],
            7: [WY(1, 1)],
        }
        post = {

            2: [W("w2", 0, 1, "S"), L("y", y_tilde, 1)],
            3: [W("w1", 1, 1, "S")],
            4: [H(0, 0), H(1, 0), H(2, 0)],
            5: [H(0, 1), H(1, 1), WY(0, 1), H(2, 1), H(3, 0)],
            6: [H(3, 1), H(4, 0), H(4, 1)],
            7: [H(5, 0), H(5, 1)],
        }
        between = {
            7: [lambda: quant_feature(6)],
        }
        spacer = {
            1: [Q("w1", 0, 0)],
            2: [Q("w2", 0, 0)],
            3: [Q("w2", 0, 1)],
            4: [Q("w1", 1, 1)],
            5: [Y(0, 1, 1)],
            6: [Q("y", 0, 1)],
            7: [Q("y", 1, 1)],
        }
        end = {
            0: [W("w1", 0, 0, "V"), W("w1", 0, 1, "S"), L("z", z_next, 0), LR("x", gate_pre, F32, 5, 1), LR("go", grad_out, BF16, 5, 1), LR("v", value, F32, 5, 1)],
            1: [Q("w1", 0, 1), LR("x", gate_pre, F32, 6, 2), LR("go", grad_out, BF16, 6, 2), LR("v", value, F32, 6, 1), spread_dt, W("w2", 0, 0, "S"), take_dt],
            3: [W("w2", 1, 0, "V"), Q("w1", 1, 0), L("z", z_next, 1), LR("v", value, F32, 7, 1), Q("w2", 1, 0)],
            4: [Y(0, 0, 0), Y(0, 0, 1), Q("w2", 1, 1), Y(0, 1, 0)],
            5: [Q("y", 0, 0)],
            6: [Y(1, 0, 0), Y(1, 0, 1), Y(1, 1, 0), Y(1, 1, 1)],
        }
        sigmoid(0, slice(0, HALF))
        sigmoid(0, slice(HALF, G))
        last = CHUNKS - 1
        for c in range(last):
            if c > 0:
                turn_d1(c - 1)
                if c > 2:
                    empty_d2(c - 1, 0)
                    empty_d2(c - 1, 1)
                empty_d1(c - 1)
            run(pre.get(c, []))
            sigmoid(c + 1)
            if c == 0:
                make_d2(c, slice(0, P))
                make_d2(c, slice(P, 2 * P))
            else:
                make_d2(c)
            run(between.get(c, []))
            make_slope(c)
            run(spacer.get(c, []))
            run(post.get(c, []))
            turn_d2(c, 0)
            turn_d2(c, 1)
            if c in (0, 1, 6):
                empty_d2(c, 0)
                empty_d2(c, 1)
            make_d1(c)
            if c > 0:
                quant_feature(c - 1)
            run(end.get(c, []))
        turn_d1(6)
        empty_d1(6)
        out_0_tile(5)
        quant_feature(6)
        out_0_tile(6)
        weave_d1(0, 0, "S")
        weave_d1(0, 1, "S")
        weave_y(1, 0, "S")
        weave_y(1, 1, "S")
        make_d2(last)
        quant_d1(0, 0, 1)
        quant_d1(1, 0, 1)
        quant_e4("y", 1, 0)
        turn_d2(last, 0)
        turn_d2(last, 1)
        make_slope(last)
        out_0_empty(5)
        for m in range(2):
            for r in range(2):
                product_1(m, r, "turn" if m == 0 else "acc", 0, 1)
        empty_d2(last, 0)
        empty_d2(last, 1)
        quant_e4("y", 1, 1)
        head, rest = slice(0, 64), slice(64, 2 * P)
        make_d1(last, head)
        make_d1(last, rest, (0,))
        weave_d1(1, 0)
        weave_d1(1, 1)
        quant_d1(0, 1, 1)
        make_d1(last, rest, (1,))
        quant_d1(1, 1, 1)
        quant_feature(last, 1, 1)
        out_0_empty(6)
        for m in range(2):
            for r in range(2):
                product_1(m, r, "", 1)
        turn_d1(last)
        product_0(last, 0, 0, 2)
        weave_d1(0, 2)
        weave_d1(1, 2)
        weave_d1(0, 3)
        quant_d1(2)
        weave_d1(1, 3)
        for m in range(2):
            for r in range(2):
                empty_1(m, r, "S")
        empty_d1(last)
        for r in range(2):
            product_1(2, r, "turn")
        product_0(last, 1, 0, 2)
        weave_d1(0, 4)
        quant_d1(3)
        for r in range(2):
            product_1(3, r, "acc")
        weave_d1(1, 4)
        for r in range(2):
            empty_1(2, r, "S")
        weave_d1(0, 5)
        quant_d1(4)
        for r in range(2):
            product_1(4, r, "turn")
        for r in range(2):
            empty_1(3, r, "S")
        for r in range(2):
            product_1(5, r, "turn")
        weave_d1(1, 5)
        quant_feature(last, 0, 1)
        quant_d1(5)
        for r in range(2):
            product_0(last, r, 2)
        for m in (4, 5):
            for r in range(2):
                empty_1(m, r, "SV"[r])
        for r in range(2):
            product_1(6, r, "turn")
        empty_0(last, 0, "S")
        empty_0(last, 1, "V")
        for r in range(2):
            product_1(7, r, "acc")
        for m in (6, 7):
            for r in range(2):
                empty_1(m, r, "SV"[r])
